import numpy as np
import ml_dtypes

BF16 = ml_dtypes.bfloat16


def bf(x):
    return np.asarray(x, np.float32).astype(BF16)


def f32(x):
    return np.asarray(x, np.float32)


def f64(x):
    return np.asarray(x).astype(np.float64)


def striped(idx):
    return np.tile(idx.reshape(-1, 16).T, (8, 1))


C, H, D, HALF, S, N = 512, 4, 128, 64, 256, 64
ROPE_BASE = 10000.0


def setup_inputs():
    k = np.random.standard_normal((H, D, N))
    k = k / np.sqrt(np.mean(np.square(k), axis=1, keepdims=True))
    ang = f32(1.0 / ROPE_BASE ** (np.arange(HALF) / HALF))[:, None] * f32(np.arange(N))[None, :]
    return {"base": f32(np.random.standard_normal((C, S))), "k": f32(k.reshape(C, N)), "w": f32(1.0 + 0.1 * np.random.standard_normal((D, 1))), "cos": f32(np.cos(f64(ang))), "sin": f32(np.sin(f64(ang))), "offs": striped(np.random.permutation(S)[:N])}


def reference(base, k, w, cos, sin, offs):
    idx = offs[:16].T.reshape(-1)
    x = f64(k).reshape(H, D, N) * f64(w)[None, :, :]
    x1, x2 = x[:, :HALF, :], x[:, HALF:, :]
    cc, ss = f64(cos)[None, :, :], f64(sin)[None, :, :]
    r = np.concatenate([x1 * cc - x2 * ss, x2 * cc + x1 * ss], axis=1).reshape(C, N)
    out = f64(base).copy()
    out[:, idx] = r
    return out

@@ -1,0 +1,63 @@
+import concourse.mybir as mybir
+
+F32 = mybir.dt.float32
+U16 = mybir.dt.uint16
+MULT = mybir.AluOpType.mult
+ADD = mybir.AluOpType.add
+
+HEADS = 4
+HEAD_DIM = 128
+HALF = 64
+TOKENS = 64
+SLOTS = 256
+
+
+def tile_qknormropekvcachetestmodel_kernel(tc, base, k, w, cos, sin, offs, out):
+    nc = tc.nc
+    lower = slice(0, HALF)
+    upper = slice(HALF, HEAD_DIM)
+    k_by_head = k.rearrange("(h e) j -> e h j", e=HEAD_DIM)
+
+    with tc.tile_pool(name="held", bufs=1) as held:
+        offsets = held.tile([HEAD_DIM, TOKENS // 16], U16, name="offsets")
+        nc.sync.dma_start(offsets[:], offs)
+
+        keys = held.tile([HEAD_DIM, HEADS, TOKENS], F32, name="keys")
+        gain = held.tile([HEAD_DIM, 1], F32, name="gain")
+        cos_both = held.tile([HEAD_DIM, TOKENS], F32, name="cos_both")
+        nc.sync.dma_start(keys[:], k_by_head)
+        nc.sync.dma_start(gain[:], w)
+        nc.sync.dma_start(cos_both[lower, :], cos)
+        nc.sync.dma_start(cos_both[upper, :], cos)
+
+        partner_keys = held.tile([HEAD_DIM, HEADS, TOKENS], F32, name="partner_keys")
+        partner_gain = held.tile([HEAD_DIM, 1], F32, name="partner_gain")
+        sin_both = held.tile([HEAD_DIM, TOKENS], F32, name="sin_both")
+        nc.scalar.dma_start(partner_keys[lower, :, :], k_by_head[upper, :, :])
+        nc.scalar.dma_start(partner_keys[upper, :, :], k_by_head[lower, :, :])
+        nc.scalar.dma_start(partner_gain[lower, :], w[upper, :])
+        nc.scalar.dma_start(partner_gain[upper, :], w[lower, :])
+        nc.scalar.dma_start(sin_both[lower, :], sin)
+        nc.scalar.dma_start(sin_both[upper, :], sin)
+
+        windows = [held.tile([HEAD_DIM, SLOTS], F32, name=f"window{h}") for h in range(HEADS)]
+        for h in range(HEADS):
+            queue = nc.sync if h % 2 == 0 else nc.scalar
+            queue.dma_start(windows[h][:], base[h * HEAD_DIM : (h + 1) * HEAD_DIM, :])
+
+        nc.vector.tensor_scalar_mul(partner_gain[lower, :], partner_gain[lower, :], -1.0)
+
+        per_head = [HEAD_DIM, HEADS, TOKENS]
+        own = held.tile(per_head, F32, name="own")
+        crossed = held.tile(per_head, F32, name="crossed")
+        nc.vector.scalar_tensor_tensor(
+            own[:], keys[:], gain[:, 0:1], cos_both[:].unsqueeze(1).to_broadcast(per_head), MULT, MULT
+        )
+        nc.vector.scalar_tensor_tensor(
+            crossed[:], partner_keys[:], partner_gain[:, 0:1], sin_both[:].unsqueeze(1).to_broadcast(per_head), MULT, MULT
+        )
+
+        for h in range(HEADS):
+            nc.vector.tensor_tensor(windows[h][:].indirect(offsets[:]), own[:, h, :], crossed[:, h, :], ADD)
+            queue = nc.sync if h % 2 == 0 else nc.scalar
+            queue.dma_start(out[h * HEAD_DIM : (h + 1) * HEAD_DIM, :], windows[h][:])

@@ -4,6 +4,7 @@ F32 = mybir.dt.float32
 U16 = mybir.dt.uint16
 MULT = mybir.AluOpType.mult
 ADD = mybir.AluOpType.add
+NOT_EQUAL = mybir.AluOpType.not_equal
 
 HEADS = 4
 HEAD_DIM = 128
@@ -17,35 +18,55 @@ def tile_qknormropekvcachetestmodel_kernel(tc, base, k, w, cos, sin, offs, out):
     lower = slice(0, HALF)
     upper = slice(HALF, HEAD_DIM)
     k_by_head = k.rearrange("(h e) j -> e h j", e=HEAD_DIM)
+    square = [HEAD_DIM, HEAD_DIM]
 
-    with tc.tile_pool(name="held", bufs=1) as held:
+    with tc.tile_pool(name="held", bufs=1) as held, tc.psum_pool(name="psum", bufs=1) as psum:
         offsets = held.tile([HEAD_DIM, TOKENS // 16], U16, name="offsets")
-        nc.sync.dma_start(offsets[:], offs)
-
-        keys = held.tile([HEAD_DIM, HEADS, TOKENS], F32, name="keys")
         gain = held.tile([HEAD_DIM, 1], F32, name="gain")
-        cos_both = held.tile([HEAD_DIM, TOKENS], F32, name="cos_both")
-        nc.sync.dma_start(keys[:], k_by_head)
-        nc.sync.dma_start(gain[:], w)
-        nc.sync.dma_start(cos_both[lower, :], cos)
-        nc.sync.dma_start(cos_both[upper, :], cos)
-
+        trig = held.tile([HEAD_DIM, TOKENS], F32, name="trig")
+        keys = held.tile([HEAD_DIM, HEADS, TOKENS], F32, name="keys")
         partner_keys = held.tile([HEAD_DIM, HEADS, TOKENS], F32, name="partner_keys")
-        partner_gain = held.tile([HEAD_DIM, 1], F32, name="partner_gain")
-        sin_both = held.tile([HEAD_DIM, TOKENS], F32, name="sin_both")
-        nc.scalar.dma_start(partner_keys[lower, :, :], k_by_head[upper, :, :])
-        nc.scalar.dma_start(partner_keys[upper, :, :], k_by_head[lower, :, :])
-        nc.scalar.dma_start(partner_gain[lower, :], w[upper, :])
-        nc.scalar.dma_start(partner_gain[upper, :], w[lower, :])
-        nc.scalar.dma_start(sin_both[lower, :], sin)
-        nc.scalar.dma_start(sin_both[upper, :], sin)
-
         windows = [held.tile([HEAD_DIM, SLOTS], F32, name=f"window{h}") for h in range(HEADS)]
+
+        nc.sync.dma_start(offsets[:], offs)
+        nc.scalar.dma_start(gain[:], w)
+        nc.sync.dma_start(trig[lower, :], cos)
+        nc.scalar.dma_start(trig[upper, :], sin)
+        nc.sync.dma_start(keys[:], k_by_head)
+        nc.scalar.dma_start(partner_keys[lower, :, :], k_by_head[upper, :, :])
+        nc.sync.dma_start(partner_keys[upper, :, :], k_by_head[lower, :, :])
         for h in range(HEADS):
-            queue = nc.sync if h % 2 == 0 else nc.scalar
+            queue = nc.scalar if h % 2 == 0 else nc.sync
             queue.dma_start(windows[h][:], base[h * HEAD_DIM : (h + 1) * HEAD_DIM, :])
 
-        nc.vector.tensor_scalar_mul(partner_gain[lower, :], partner_gain[lower, :], -1.0)
+        swap = held.tile(square, F32, name="swap")
+        spread_lower = held.tile(square, F32, name="spread_lower")
+        spread_upper = held.tile(square, F32, name="spread_upper")
+        for matrix in (swap, spread_lower, spread_upper):
+            nc.vector.memset(matrix[:], 0.0)
+        nc.gpsimd.affine_select(
+            out=swap[:], in_=swap[:], pattern=[[-1, HEAD_DIM]], compare_op=NOT_EQUAL, fill=-1.0,
+            base=-HALF, channel_multiplier=1,
+        )
+        nc.gpsimd.affine_select(
+            out=swap[:], in_=swap[:], pattern=[[-1, HEAD_DIM]], compare_op=NOT_EQUAL, fill=1.0,
+            base=HALF, channel_multiplier=1,
+        )
+        nc.gpsimd.affine_select(
+            out=spread_lower[:], in_=spread_lower[:], pattern=[[0, 2], [-1, HALF]], compare_op=NOT_EQUAL, fill=1.0,
+            base=0, channel_multiplier=1,
+        )
+        nc.gpsimd.affine_select(
+            out=spread_upper[:], in_=spread_upper[:], pattern=[[0, 2], [-1, HALF]], compare_op=NOT_EQUAL, fill=1.0,
+            base=-HALF, channel_multiplier=1,
+        )
+
+        partner_gain = psum.tile([HEAD_DIM, 1], F32, name="partner_gain")
+        cos_both = psum.tile([HEAD_DIM, TOKENS], F32, name="cos_both")
+        sin_both = psum.tile([HEAD_DIM, TOKENS], F32, name="sin_both")
+        nc.tensor.matmul(partner_gain[:], swap[:], gain[:])
+        nc.tensor.matmul(cos_both[:], spread_lower[:], trig[:])
+        nc.tensor.matmul(sin_both[:], spread_upper[:], trig[:])
 
         per_head = [HEAD_DIM, HEADS, TOKENS]
         own = held.tile(per_head, F32, name="own")

@@ -23,15 +23,15 @@ def tile_qknormropekvcachetestmodel_kernel(tc, base, k, w, cos, sin, offs, out):
     with tc.tile_pool(name="held", bufs=1) as held, tc.psum_pool(name="psum", bufs=1) as psum:
         offsets = held.tile([HEAD_DIM, TOKENS // 16], U16, name="offsets")
         gain = held.tile([HEAD_DIM, 1], F32, name="gain")
-        trig = held.tile([HEAD_DIM, TOKENS], F32, name="trig")
+        trig = held.tile([HEAD_DIM, 2, TOKENS], F32, name="trig")
         keys = held.tile([HEAD_DIM, HEADS, TOKENS], F32, name="keys")
         partner_keys = held.tile([HEAD_DIM, HEADS, TOKENS], F32, name="partner_keys")
         windows = [held.tile([HEAD_DIM, SLOTS], F32, name=f"window{h}") for h in range(HEADS)]
 
-        nc.sync.dma_start(offsets[:], offs)
+        nc.sync.dma_start(trig[lower, 0, :], cos)
+        nc.scalar.dma_start(trig[lower, 1, :], sin)
         nc.scalar.dma_start(gain[:], w)
-        nc.sync.dma_start(trig[lower, :], cos)
-        nc.scalar.dma_start(trig[upper, :], sin)
+        nc.sync.dma_start(offsets[:], offs)
         nc.sync.dma_start(keys[:], k_by_head)
         nc.scalar.dma_start(partner_keys[lower, :, :], k_by_head[upper, :, :])
         nc.sync.dma_start(partner_keys[upper, :, :], k_by_head[lower, :, :])
@@ -39,11 +39,15 @@ def tile_qknormropekvcachetestmodel_kernel(tc, base, k, w, cos, sin, offs, out):
             queue = nc.scalar if h % 2 == 0 else nc.sync
             queue.dma_start(windows[h][:], base[h * HEAD_DIM : (h + 1) * HEAD_DIM, :])
 
+        spread = held.tile(square, F32, name="spread")
         swap = held.tile(square, F32, name="swap")
-        spread_lower = held.tile(square, F32, name="spread_lower")
-        spread_upper = held.tile(square, F32, name="spread_upper")
-        for matrix in (swap, spread_lower, spread_upper):
-            nc.vector.memset(matrix[:], 0.0)
+        nc.vector.memset(spread[:], 0.0)
+        nc.vector.memset(swap[:], 0.0)
+        nc.vector.memset(trig[upper, :, :], 0.0)
+        nc.gpsimd.affine_select(
+            out=spread[:], in_=spread[:], pattern=[[0, 2], [-1, HALF]], compare_op=NOT_EQUAL, fill=1.0,
+            base=0, channel_multiplier=1,
+        )
         nc.gpsimd.affine_select(
             out=swap[:], in_=swap[:], pattern=[[-1, HEAD_DIM]], compare_op=NOT_EQUAL, fill=-1.0,
             base=-HALF, channel_multiplier=1,
@@ -52,30 +56,20 @@ def tile_qknormropekvcachetestmodel_kernel(tc, base, k, w, cos, sin, offs, out):
             out=swap[:], in_=swap[:], pattern=[[-1, HEAD_DIM]], compare_op=NOT_EQUAL, fill=1.0,
             base=HALF, channel_multiplier=1,
         )
-        nc.gpsimd.affine_select(
-            out=spread_lower[:], in_=spread_lower[:], pattern=[[0, 2], [-1, HALF]], compare_op=NOT_EQUAL, fill=1.0,
-            base=0, channel_multiplier=1,
-        )
-        nc.gpsimd.affine_select(
-            out=spread_upper[:], in_=spread_upper[:], pattern=[[0, 2], [-1, HALF]], compare_op=NOT_EQUAL, fill=1.0,
-            base=-HALF, channel_multiplier=1,
-        )
 
+        trig_both = psum.tile([HEAD_DIM, 2, TOKENS], F32, name="trig_both")
         partner_gain = psum.tile([HEAD_DIM, 1], F32, name="partner_gain")
-        cos_both = psum.tile([HEAD_DIM, TOKENS], F32, name="cos_both")
-        sin_both = psum.tile([HEAD_DIM, TOKENS], F32, name="sin_both")
+        nc.tensor.matmul(trig_both[:], spread[:], trig[:])
         nc.tensor.matmul(partner_gain[:], swap[:], gain[:])
-        nc.tensor.matmul(cos_both[:], spread_lower[:], trig[:])
-        nc.tensor.matmul(sin_both[:], spread_upper[:], trig[:])
 
         per_head = [HEAD_DIM, HEADS, TOKENS]
         own = held.tile(per_head, F32, name="own")
         crossed = held.tile(per_head, F32, name="crossed")
         nc.vector.scalar_tensor_tensor(
-            own[:], keys[:], gain[:, 0:1], cos_both[:].unsqueeze(1).to_broadcast(per_head), MULT, MULT
+            own[:], keys[:], gain[:, 0:1], trig_both[:, 0:1, :].to_broadcast(per_head), MULT, MULT
         )
         nc.vector.scalar_tensor_tensor(
-            crossed[:], partner_keys[:], partner_gain[:, 0:1], sin_both[:].unsqueeze(1).to_broadcast(per_head), MULT, MULT
+            crossed[:], partner_keys[:], partner_gain[:, 0:1], trig_both[:, 1:2, :].to_broadcast(per_head), MULT, MULT
         )
 
         for h in range(HEADS):

@@ -29,15 +29,14 @@ def tile_qknormropekvcachetestmodel_kernel(tc, base, k, w, cos, sin, offs, out):
         windows = [held.tile([HEAD_DIM, SLOTS], F32, name=f"window{h}") for h in range(HEADS)]
 
         nc.sync.dma_start(trig[lower, 0, :], cos)
-        nc.scalar.dma_start(trig[lower, 1, :], sin)
-        nc.scalar.dma_start(gain[:], w)
-        nc.sync.dma_start(offsets[:], offs)
+        nc.sync.dma_start(trig[lower, 1, :], sin)
+        nc.sync.dma_start(gain[:], w)
         nc.sync.dma_start(keys[:], k_by_head)
-        nc.scalar.dma_start(partner_keys[lower, :, :], k_by_head[upper, :, :])
+        nc.sync.dma_start(partner_keys[lower, :, :], k_by_head[upper, :, :])
         nc.sync.dma_start(partner_keys[upper, :, :], k_by_head[lower, :, :])
+        nc.sync.dma_start(offsets[:], offs)
         for h in range(HEADS):
-            queue = nc.scalar if h % 2 == 0 else nc.sync
-            queue.dma_start(windows[h][:], base[h * HEAD_DIM : (h + 1) * HEAD_DIM, :])
+            nc.sync.dma_start(windows[h][:], base[h * HEAD_DIM : (h + 1) * HEAD_DIM, :])
 
         spread = held.tile(square, F32, name="spread")
         swap = held.tile(square, F32, name="swap")
@@ -74,5 +73,4 @@ def tile_qknormropekvcachetestmodel_kernel(tc, base, k, w, cos, sin, offs, out):
 
         for h in range(HEADS):
             nc.vector.tensor_tensor(windows[h][:].indirect(offsets[:]), own[:, h, :], crossed[:, h, :], ADD)
-            queue = nc.sync if h % 2 == 0 else nc.scalar
-            queue.dma_start(out[h * HEAD_DIM : (h + 1) * HEAD_DIM, :], windows[h][:])
+            nc.scalar.dma_start(out[h * HEAD_DIM : (h + 1) * HEAD_DIM, :], windows[h][:])

@@ -4,73 +4,61 @@ F32 = mybir.dt.float32
 U16 = mybir.dt.uint16
 MULT = mybir.AluOpType.mult
 ADD = mybir.AluOpType.add
-NOT_EQUAL = mybir.AluOpType.not_equal
 
-HEADS = 4
-HEAD_DIM = 128
-HALF = 64
+PARTITIONS = 128
+FREQS = 64
+OUTER = 2
+INNER = 2
+HALVES = 2
 TOKENS = 64
 SLOTS = 256
 
 
 def tile_qknormropekvcachetestmodel_kernel(tc, base, k, w, cos, sin, offs, out):
     nc = tc.nc
-    lower = slice(0, HALF)
-    upper = slice(HALF, HEAD_DIM)
-    k_by_head = k.rearrange("(h e) j -> e h j", e=HEAD_DIM)
-    square = [HEAD_DIM, HEAD_DIM]
+    blocks = INNER * HALVES
 
-    with tc.tile_pool(name="held", bufs=1) as held, tc.psum_pool(name="psum", bufs=1) as psum:
-        offsets = held.tile([HEAD_DIM, TOKENS // 16], U16, name="offsets")
-        gain = held.tile([HEAD_DIM, 1], F32, name="gain")
-        trig = held.tile([HEAD_DIM, 2, TOKENS], F32, name="trig")
-        keys = held.tile([HEAD_DIM, HEADS, TOKENS], F32, name="keys")
-        partner_keys = held.tile([HEAD_DIM, HEADS, TOKENS], F32, name="partner_keys")
-        windows = [held.tile([HEAD_DIM, SLOTS], F32, name=f"window{h}") for h in range(HEADS)]
+    def by_partition(rows):
+        return rows.rearrange("(a m d) n -> d a m n", a=OUTER, m=blocks, d=FREQS)
 
-        nc.sync.dma_start(trig[lower, 0, :], cos)
-        nc.sync.dma_start(trig[lower, 1, :], sin)
-        nc.sync.dma_start(gain[:], w)
-        nc.sync.dma_start(keys[:], k_by_head)
-        nc.sync.dma_start(partner_keys[lower, :, :], k_by_head[upper, :, :])
-        nc.sync.dma_start(partner_keys[upper, :, :], k_by_head[lower, :, :])
+    def on_both(table):
+        return table.unsqueeze(1).broadcast_to([FREQS, OUTER, table.shape[1]])
+
+    with tc.tile_pool(name="held", bufs=1) as held:
+        offsets = held.tile([PARTITIONS, TOKENS // 16], U16, name="offsets")
+        gain_lower = held.tile([PARTITIONS, 1], F32, name="gain_lower")
+        gain_upper = held.tile([PARTITIONS, 1], F32, name="gain_upper")
+        minus_gain_upper = held.tile([PARTITIONS, 1], F32, name="minus_gain_upper")
+        cosine = held.tile([PARTITIONS, TOKENS], F32, name="cosine")
+        sine = held.tile([PARTITIONS, TOKENS], F32, name="sine")
+        keys = held.tile([PARTITIONS, INNER, HALVES, TOKENS], F32, name="keys")
+        windows = [
+            [held.tile([PARTITIONS, SLOTS], F32, name=f"window{g}{s}") for s in range(HALVES)] for g in range(INNER)
+        ]
+
+        nc.sync.dma_start(cosine[:], on_both(cos))
+        nc.sync.dma_start(gain_lower[:], on_both(w[0:FREQS, :]))
+        nc.sync.dma_start(keys[:], k.rearrange("(q d) j -> d q j", d=FREQS))
+        nc.sync.dma_start(sine[:], on_both(sin))
+        nc.sync.dma_start(gain_upper[:], on_both(w[FREQS : 2 * FREQS, :]))
         nc.sync.dma_start(offsets[:], offs)
-        for h in range(HEADS):
-            nc.sync.dma_start(windows[h][:], base[h * HEAD_DIM : (h + 1) * HEAD_DIM, :])
+        for s in range(HALVES):
+            for g in range(INNER):
+                nc.sync.dma_start(windows[g][s][:], by_partition(base)[:, :, HALVES * g + s, :])
 
-        spread = held.tile(square, F32, name="spread")
-        swap = held.tile(square, F32, name="swap")
-        nc.vector.memset(spread[:], 0.0)
-        nc.vector.memset(swap[:], 0.0)
-        nc.vector.memset(trig[upper, :, :], 0.0)
-        nc.gpsimd.affine_select(
-            out=spread[:], in_=spread[:], pattern=[[0, 2], [-1, HALF]], compare_op=NOT_EQUAL, fill=1.0,
-            base=0, channel_multiplier=1,
-        )
-        nc.gpsimd.affine_select(
-            out=swap[:], in_=swap[:], pattern=[[-1, HEAD_DIM]], compare_op=NOT_EQUAL, fill=-1.0,
-            base=-HALF, channel_multiplier=1,
-        )
-        nc.gpsimd.affine_select(
-            out=swap[:], in_=swap[:], pattern=[[-1, HEAD_DIM]], compare_op=NOT_EQUAL, fill=1.0,
-            base=HALF, channel_multiplier=1,
-        )
+        nc.gpsimd.tensor_scalar(minus_gain_upper[:], gain_upper[:], -1.0, None, MULT)
 
-        trig_both = psum.tile([HEAD_DIM, 2, TOKENS], F32, name="trig_both")
-        partner_gain = psum.tile([HEAD_DIM, 1], F32, name="partner_gain")
-        nc.tensor.matmul(trig_both[:], spread[:], trig[:])
-        nc.tensor.matmul(partner_gain[:], swap[:], gain[:])
+        both_heads = [PARTITIONS, INNER, TOKENS]
+        own = [held.tile(both_heads, F32, name=f"own{s}") for s in range(HALVES)]
+        crossed = [held.tile(both_heads, F32, name=f"crossed{s}") for s in range(HALVES)]
+        cosine_both = cosine[:].unsqueeze(1).to_broadcast(both_heads)
+        sine_both = sine[:].unsqueeze(1).to_broadcast(both_heads)
+        nc.vector.scalar_tensor_tensor(own[0][:], keys[:, :, 0, :], gain_lower[:, 0:1], cosine_both, MULT, MULT)
+        nc.vector.scalar_tensor_tensor(crossed[1][:], keys[:, :, 0, :], gain_lower[:, 0:1], sine_both, MULT, MULT)
+        nc.vector.scalar_tensor_tensor(own[1][:], keys[:, :, 1, :], gain_upper[:, 0:1], cosine_both, MULT, MULT)
+        nc.vector.scalar_tensor_tensor(crossed[0][:], keys[:, :, 1, :], minus_gain_upper[:, 0:1], sine_both, MULT, MULT)
 
-        per_head = [HEAD_DIM, HEADS, TOKENS]
-        own = held.tile(per_head, F32, name="own")
-        crossed = held.tile(per_head, F32, name="crossed")
-        nc.vector.scalar_tensor_tensor(
-            own[:], keys[:], gain[:, 0:1], trig_both[:, 0:1, :].to_broadcast(per_head), MULT, MULT
-        )
-        nc.vector.scalar_tensor_tensor(
-            crossed[:], partner_keys[:], partner_gain[:, 0:1], trig_both[:, 1:2, :].to_broadcast(per_head), MULT, MULT
-        )
-
-        for h in range(HEADS):
-            nc.vector.tensor_tensor(windows[h][:].indirect(offsets[:]), own[:, h, :], crossed[:, h, :], ADD)
-            nc.scalar.dma_start(out[h * HEAD_DIM : (h + 1) * HEAD_DIM, :], windows[h][:])
+        for s in range(HALVES):
+            for g in range(INNER):
+                nc.vector.tensor_tensor(windows[g][s][:].indirect(offsets[:]), own[s][:, g, :], crossed[s][:, g, :], ADD)
+                nc.scalar.dma_start(by_partition(out)[:, :, HALVES * g + s, :], windows[g][s][:])

@@ -42,11 +42,12 @@ def tile_qknormropekvcachetestmodel_kernel(tc, base, k, w, cos, sin, offs, out):
         nc.sync.dma_start(sine[:], on_both(sin))
         nc.sync.dma_start(gain_upper[:], on_both(w[FREQS : 2 * FREQS, :]))
         nc.sync.dma_start(offsets[:], offs)
+        window_queue = [nc.sync, nc.gpsimd]
         for s in range(HALVES):
             for g in range(INNER):
-                nc.sync.dma_start(windows[g][s][:], by_partition(base)[:, :, HALVES * g + s, :])
+                window_queue[s].dma_start(windows[g][s][:], by_partition(base)[:, :, HALVES * g + s, :])
 
-        nc.gpsimd.tensor_scalar(minus_gain_upper[:], gain_upper[:], -1.0, None, MULT)
+        nc.vector.tensor_scalar(minus_gain_upper[:], gain_upper[:], -1.0, None, MULT)
 
         both_heads = [PARTITIONS, INNER, TOKENS]
         own = [held.tile(both_heads, F32, name=f"own{s}") for s in range(HALVES)]

@@ -36,11 +36,11 @@ def tile_qknormropekvcachetestmodel_kernel(tc, base, k, w, cos, sin, offs, out):
             [held.tile([PARTITIONS, SLOTS], F32, name=f"window{g}{s}") for s in range(HALVES)] for g in range(INNER)
         ]
 
-        nc.sync.dma_start(cosine[:], on_both(cos))
+        nc.sync.dma_start(gain_upper[:], on_both(w[FREQS : 2 * FREQS, :]))
         nc.sync.dma_start(gain_lower[:], on_both(w[0:FREQS, :]))
         nc.sync.dma_start(keys[:], k.rearrange("(q d) j -> d q j", d=FREQS))
+        nc.sync.dma_start(cosine[:], on_both(cos))
         nc.sync.dma_start(sine[:], on_both(sin))
-        nc.sync.dma_start(gain_upper[:], on_both(w[FREQS : 2 * FREQS, :]))
         nc.sync.dma_start(offsets[:], offs)
         window_queue = [nc.sync, nc.gpsimd]
         for s in range(HALVES):

@@ -24,6 +24,9 @@ def tile_qknormropekvcachetestmodel_kernel(tc, base, k, w, cos, sin, offs, out):
     def on_both(table):
         return table.unsqueeze(1).broadcast_to([FREQS, OUTER, table.shape[1]])
 
+    def half_of_keys(s):
+        return k.rearrange("(h s d) j -> d h s j", h=OUTER * INNER, s=HALVES, d=FREQS)[:, :, s, :]
+
     with tc.tile_pool(name="held", bufs=1) as held:
         offsets = held.tile([PARTITIONS, TOKENS // 16], U16, name="offsets")
         gain_lower = held.tile([PARTITIONS, 1], F32, name="gain_lower")
@@ -31,35 +34,40 @@ def tile_qknormropekvcachetestmodel_kernel(tc, base, k, w, cos, sin, offs, out):
         minus_gain_upper = held.tile([PARTITIONS, 1], F32, name="minus_gain_upper")
         cosine = held.tile([PARTITIONS, TOKENS], F32, name="cosine")
         sine = held.tile([PARTITIONS, TOKENS], F32, name="sine")
-        keys = held.tile([PARTITIONS, INNER, HALVES, TOKENS], F32, name="keys")
+        both_heads = [PARTITIONS, INNER, TOKENS]
+        keys_lower = held.tile(both_heads, F32, name="keys_lower")
+        keys_upper = held.tile(both_heads, F32, name="keys_upper")
         windows = [
             [held.tile([PARTITIONS, SLOTS], F32, name=f"window{g}{s}") for s in range(HALVES)] for g in range(INNER)
         ]
 
-        nc.sync.dma_start(gain_upper[:], on_both(w[FREQS : 2 * FREQS, :]))
-        nc.sync.dma_start(gain_lower[:], on_both(w[0:FREQS, :]))
-        nc.sync.dma_start(keys[:], k.rearrange("(q d) j -> d q j", d=FREQS))
         nc.sync.dma_start(cosine[:], on_both(cos))
+        nc.sync.dma_start(gain_lower[:], on_both(w[0:FREQS, :]))
+        nc.sync.dma_start(keys_lower[:], half_of_keys(0))
         nc.sync.dma_start(sine[:], on_both(sin))
+        nc.sync.dma_start(gain_upper[:], on_both(w[FREQS : 2 * FREQS, :]))
+        nc.sync.dma_start(keys_upper[:], half_of_keys(1))
         nc.sync.dma_start(offsets[:], offs)
-        window_queue = [nc.sync, nc.gpsimd]
-        for s in range(HALVES):
-            for g in range(INNER):
-                window_queue[s].dma_start(windows[g][s][:], by_partition(base)[:, :, HALVES * g + s, :])
+        nc.gpsimd.dma_start(windows[0][1][:], by_partition(base)[:, :, 1, :])
+        nc.sync.dma_start(windows[1][1][:], by_partition(base)[:, :, 3, :])
+        nc.sync.dma_start(windows[0][0][:], by_partition(base)[:, :, 0, :])
+        nc.sync.dma_start(windows[1][0][:], by_partition(base)[:, :, 2, :])
 
-        nc.vector.tensor_scalar(minus_gain_upper[:], gain_upper[:], -1.0, None, MULT)
-
-        both_heads = [PARTITIONS, INNER, TOKENS]
         own = [held.tile(both_heads, F32, name=f"own{s}") for s in range(HALVES)]
         crossed = [held.tile(both_heads, F32, name=f"crossed{s}") for s in range(HALVES)]
         cosine_both = cosine[:].unsqueeze(1).to_broadcast(both_heads)
         sine_both = sine[:].unsqueeze(1).to_broadcast(both_heads)
-        nc.vector.scalar_tensor_tensor(own[0][:], keys[:, :, 0, :], gain_lower[:, 0:1], cosine_both, MULT, MULT)
-        nc.vector.scalar_tensor_tensor(crossed[1][:], keys[:, :, 0, :], gain_lower[:, 0:1], sine_both, MULT, MULT)
-        nc.vector.scalar_tensor_tensor(own[1][:], keys[:, :, 1, :], gain_upper[:, 0:1], cosine_both, MULT, MULT)
-        nc.vector.scalar_tensor_tensor(crossed[0][:], keys[:, :, 1, :], minus_gain_upper[:, 0:1], sine_both, MULT, MULT)
+        nc.vector.scalar_tensor_tensor(own[0][:], keys_lower[:], gain_lower[:, 0:1], cosine_both, MULT, MULT)
+        nc.vector.scalar_tensor_tensor(crossed[1][:], keys_lower[:], gain_lower[:, 0:1], sine_both, MULT, MULT)
+        nc.vector.tensor_scalar(minus_gain_upper[:], gain_upper[:], -1.0, None, MULT)
+        nc.vector.scalar_tensor_tensor(own[1][:], keys_upper[:], gain_upper[:, 0:1], cosine_both, MULT, MULT)
+        nc.vector.scalar_tensor_tensor(crossed[0][:], keys_upper[:], minus_gain_upper[:, 0:1], sine_both, MULT, MULT)
 
-        for s in range(HALVES):
-            for g in range(INNER):
-                nc.vector.tensor_tensor(windows[g][s][:].indirect(offsets[:]), own[s][:, g, :], crossed[s][:, g, :], ADD)
-                nc.scalar.dma_start(by_partition(out)[:, :, HALVES * g + s, :], windows[g][s][:])
+        nc.vector.tensor_tensor(windows[0][1][:].indirect(offsets[:]), own[1][:, 0, :], crossed[1][:, 0, :], ADD)
+        nc.scalar.dma_start(by_partition(out)[:, :, 1, :], windows[0][1][:])
+        nc.vector.tensor_tensor(windows[1][1][:].indirect(offsets[:]), own[1][:, 1, :], crossed[1][:, 1, :], ADD)
+        nc.scalar.dma_start(by_partition(out)[:, :, 3, :], windows[1][1][:])
+        nc.vector.tensor_tensor(windows[0][0][:].indirect(offsets[:]), own[0][:, 0, :], crossed[0][:, 0, :], ADD)
+        nc.scalar.dma_start(by_partition(out)[:, :, 0, :], windows[0][0][:])
+        nc.vector.tensor_tensor(windows[1][0][:].indirect(offsets[:]), own[0][:, 1, :], crossed[0][:, 1, :], ADD)
+        nc.scalar.dma_start(by_partition(out)[:, :, 2, :], windows[1][0][:])

@@ -41,11 +41,11 @@ def tile_qknormropekvcachetestmodel_kernel(tc, base, k, w, cos, sin, offs, out):
             [held.tile([PARTITIONS, SLOTS], F32, name=f"window{g}{s}") for s in range(HALVES)] for g in range(INNER)
         ]
 
+        nc.scalar.dma_start(gain_lower[:], on_both(w[0:FREQS, :]))
+        nc.scalar.dma_start(gain_upper[:], on_both(w[FREQS : 2 * FREQS, :]))
         nc.sync.dma_start(cosine[:], on_both(cos))
-        nc.sync.dma_start(gain_lower[:], on_both(w[0:FREQS, :]))
         nc.sync.dma_start(keys_lower[:], half_of_keys(0))
         nc.sync.dma_start(sine[:], on_both(sin))
-        nc.sync.dma_start(gain_upper[:], on_both(w[FREQS : 2 * FREQS, :]))
         nc.sync.dma_start(keys_upper[:], half_of_keys(1))
         nc.sync.dma_start(offsets[:], offs)
         nc.gpsimd.dma_start(windows[0][1][:], by_partition(base)[:, :, 1, :])

@@ -41,14 +41,14 @@ def tile_qknormropekvcachetestmodel_kernel(tc, base, k, w, cos, sin, offs, out):
             [held.tile([PARTITIONS, SLOTS], F32, name=f"window{g}{s}") for s in range(HALVES)] for g in range(INNER)
         ]
 
+        nc.sync.dma_start(cosine[:], on_both(cos))
         nc.scalar.dma_start(gain_lower[:], on_both(w[0:FREQS, :]))
         nc.scalar.dma_start(gain_upper[:], on_both(w[FREQS : 2 * FREQS, :]))
-        nc.sync.dma_start(cosine[:], on_both(cos))
         nc.sync.dma_start(keys_lower[:], half_of_keys(0))
         nc.sync.dma_start(sine[:], on_both(sin))
         nc.sync.dma_start(keys_upper[:], half_of_keys(1))
         nc.sync.dma_start(offsets[:], offs)
-        nc.gpsimd.dma_start(windows[0][1][:], by_partition(base)[:, :, 1, :])
+        nc.sync.dma_start(windows[0][1][:], by_partition(base)[:, :, 1, :])
         nc.sync.dma_start(windows[1][1][:], by_partition(base)[:, :, 3, :])
         nc.sync.dma_start(windows[0][0][:], by_partition(base)[:, :, 0, :])
         nc.sync.dma_start(windows[1][0][:], by_partition(base)[:, :, 2, :])

@@ -12,6 +12,7 @@ INNER = 2
 HALVES = 2
 TOKENS = 64
 SLOTS = 256
+BUS_BYTES = 256
 
 
 def tile_qknormropekvcachetestmodel_kernel(tc, base, k, w, cos, sin, offs, out):
@@ -32,13 +33,14 @@ def tile_qknormropekvcachetestmodel_kernel(tc, base, k, w, cos, sin, offs, out):
         gain_lower = held.tile([PARTITIONS, 1], F32, name="gain_lower")
         gain_upper = held.tile([PARTITIONS, 1], F32, name="gain_upper")
         minus_gain_upper = held.tile([PARTITIONS, 1], F32, name="minus_gain_upper")
-        cosine = held.tile([PARTITIONS, TOKENS], F32, name="cosine")
-        sine = held.tile([PARTITIONS, TOKENS], F32, name="sine")
+        cosine = held.tile([PARTITIONS, TOKENS], F32, name="cosine", align_bytes=BUS_BYTES)
+        sine = held.tile([PARTITIONS, TOKENS], F32, name="sine", align_bytes=BUS_BYTES)
         both_heads = [PARTITIONS, INNER, TOKENS]
-        keys_lower = held.tile(both_heads, F32, name="keys_lower")
-        keys_upper = held.tile(both_heads, F32, name="keys_upper")
+        keys_lower = held.tile(both_heads, F32, name="keys_lower", align_bytes=BUS_BYTES)
+        keys_upper = held.tile(both_heads, F32, name="keys_upper", align_bytes=BUS_BYTES)
         windows = [
-            [held.tile([PARTITIONS, SLOTS], F32, name=f"window{g}{s}") for s in range(HALVES)] for g in range(INNER)
+            [held.tile([PARTITIONS, SLOTS], F32, name=f"window{g}{s}", align_bytes=BUS_BYTES) for s in range(HALVES)]
+            for g in range(INNER)
         ]
 
         nc.sync.dma_start(cosine[:], on_both(cos))

import concourse.mybir as mybir

F32 = mybir.dt.float32
U16 = mybir.dt.uint16
MULT = mybir.AluOpType.mult
ADD = mybir.AluOpType.add

PARTITIONS = 128
FREQS = 64
OUTER = 2
INNER = 2
HALVES = 2
TOKENS = 64
SLOTS = 256
BUS_BYTES = 256


def tile_qknormropekvcachetestmodel_kernel(tc, base, k, w, cos, sin, offs, out):
    nc = tc.nc
    blocks = INNER * HALVES

    def by_partition(rows):
        return rows.rearrange("(a m d) n -> d a m n", a=OUTER, m=blocks, d=FREQS)

    def on_both(table):
        return table.unsqueeze(1).broadcast_to([FREQS, OUTER, table.shape[1]])

    def half_of_keys(s):
        return k.rearrange("(h s d) j -> d h s j", h=OUTER * INNER, s=HALVES, d=FREQS)[:, :, s, :]

    with tc.tile_pool(name="held", bufs=1) as held:
        offsets = held.tile([PARTITIONS, TOKENS // 16], U16, name="offsets")
        gain_lower = held.tile([PARTITIONS, 1], F32, name="gain_lower")
        gain_upper = held.tile([PARTITIONS, 1], F32, name="gain_upper")
        minus_gain_upper = held.tile([PARTITIONS, 1], F32, name="minus_gain_upper")
        cosine = held.tile([PARTITIONS, TOKENS], F32, name="cosine", align_bytes=BUS_BYTES)
        sine = held.tile([PARTITIONS, TOKENS], F32, name="sine", align_bytes=BUS_BYTES)
        both_heads = [PARTITIONS, INNER, TOKENS]
        keys_lower = held.tile(both_heads, F32, name="keys_lower", align_bytes=BUS_BYTES)
        keys_upper = held.tile(both_heads, F32, name="keys_upper", align_bytes=BUS_BYTES)
        windows = [
            [held.tile([PARTITIONS, SLOTS], F32, name=f"window{g}{s}", align_bytes=BUS_BYTES) for s in range(HALVES)]
            for g in range(INNER)
        ]

        nc.sync.dma_start(cosine[:], on_both(cos))
        nc.scalar.dma_start(gain_lower[:], on_both(w[0:FREQS, :]))
        nc.scalar.dma_start(gain_upper[:], on_both(w[FREQS : 2 * FREQS, :]))
        nc.sync.dma_start(keys_lower[:], half_of_keys(0))
        nc.sync.dma_start(sine[:], on_both(sin))
        nc.sync.dma_start(keys_upper[:], half_of_keys(1))
        nc.sync.dma_start(offsets[:], offs)
        nc.sync.dma_start(windows[0][1][:], by_partition(base)[:, :, 1, :])
        nc.sync.dma_start(windows[1][1][:], by_partition(base)[:, :, 3, :])
        nc.sync.dma_start(windows[0][0][:], by_partition(base)[:, :, 0, :])
        nc.sync.dma_start(windows[1][0][:], by_partition(base)[:, :, 2, :])

        own = [held.tile(both_heads, F32, name=f"own{s}") for s in range(HALVES)]
        crossed = [held.tile(both_heads, F32, name=f"crossed{s}") for s in range(HALVES)]
        cosine_both = cosine[:].unsqueeze(1).to_broadcast(both_heads)
        sine_both = sine[:].unsqueeze(1).to_broadcast(both_heads)
        nc.vector.scalar_tensor_tensor(own[0][:], keys_lower[:], gain_lower[:, 0:1], cosine_both, MULT, MULT)
        nc.vector.scalar_tensor_tensor(crossed[1][:], keys_lower[:], gain_lower[:, 0:1], sine_both, MULT, MULT)
        nc.vector.tensor_scalar(minus_gain_upper[:], gain_upper[:], -1.0, None, MULT)
        nc.vector.scalar_tensor_tensor(own[1][:], keys_upper[:], gain_upper[:, 0:1], cosine_both, MULT, MULT)
        nc.vector.scalar_tensor_tensor(crossed[0][:], keys_upper[:], minus_gain_upper[:, 0:1], sine_both, MULT, MULT)

        nc.vector.tensor_tensor(windows[0][1][:].indirect(offsets[:]), own[1][:, 0, :], crossed[1][:, 0, :], ADD)
        nc.scalar.dma_start(by_partition(out)[:, :, 1, :], windows[0][1][:])
        nc.vector.tensor_tensor(windows[1][1][:].indirect(offsets[:]), own[1][:, 1, :], crossed[1][:, 1, :], ADD)
        nc.scalar.dma_start(by_partition(out)[:, :, 3, :], windows[1][1][:])
        nc.vector.tensor_tensor(windows[0][0][:].indirect(offsets[:]), own[0][:, 0, :], crossed[0][:, 0, :], ADD)
        nc.scalar.dma_start(by_partition(out)[:, :, 0, :], windows[0][0][:])
        nc.vector.tensor_tensor(windows[1][0][:].indirect(offsets[:]), own[0][:, 1, :], crossed[0][:, 1, :], ADD)
        nc.scalar.dma_start(by_partition(out)[:, :, 2, :], windows[1][0][:])
